import numpy as np
import ml_dtypes


def mxq(x, axis, fmt="e4m3"):
    dtype, down = {"e4m3": (ml_dtypes.float8_e4m3fn, 7), "e5m2": (ml_dtypes.float8_e5m2, 14)}[fmt]
    v = np.moveaxis(np.asarray(x, np.float32).astype(ml_dtypes.bfloat16).astype(np.float64), axis, -1)
    blocks = v.reshape(v.shape[:-1] + (-1, 32))
    amax = np.abs(blocks).max(-1, keepdims=True)
    byte = np.maximum(np.where(amax > 0, np.frexp(amax)[1] - 1 + 127, 0) - down, 1)
    scale = np.exp2(byte - 127.0)
    codes = (blocks / scale).astype(np.float32).astype(dtype).astype(np.float64)
    return np.moveaxis((codes * scale).reshape(v.shape), -1, axis)


WIDE = False


def mx_kscale(k):
    if not WIDE:
        return np.ones(k)
    levels = np.array([10, -10, 5, -5, 0])
    a = np.random.permutation(np.resize(levels, k // 512 * 4)).reshape(k // 512, 4)
    idx = np.arange(k)
    return np.exp2(a[idx // 512, idx % 128 // 32])


BF16 = ml_dtypes.bfloat16


def bf(x):
    return np.asarray(x, np.float32).astype(BF16)


def f64(x):
    return np.asarray(x).astype(np.float64)


B, NH, HD, H, W = 1, 2, 512, 16, 256
NEG_INF = -1e9


def setup_inputs():
    s = mx_kscale(HD)[None, None, :, None, None]
    a = 1.3 / HD ** 0.25
    return {"q": bf(np.random.standard_normal((B, NH, HD, H, W)) * a * s),
            "k": bf(np.random.standard_normal((B, NH, HD, H, W)) * a / s)}


def reference(q, k):
    qq = mxq(f64(q), 2, "e4m3")
    kq = mxq(f64(k), 2, "e4m3")
    e_h = (qq.transpose(0, 1, 4, 3, 2) @ kq.transpose(0, 1, 4, 2, 3)).transpose(0, 1, 3, 2, 4)
    e_h = np.where(np.eye(H, dtype=bool)[:, None, :], NEG_INF, e_h)
    e_w = qq.transpose(0, 1, 3, 4, 2) @ kq.transpose(0, 1, 3, 2, 4)
    e = np.concatenate([e_h, e_w], axis=-1)
    p = np.exp(e - e.max(-1, keepdims=True))
    return p / p.sum(-1, keepdims=True)

@@ -1,0 +1,230 @@
+import concourse.mybir as mybir
+
+BF16 = mybir.dt.bfloat16
+F32 = mybir.dt.float32
+I32 = mybir.dt.int32
+U32 = mybir.dt.uint32
+U8 = mybir.dt.uint8
+FP8X4 = mybir.dt.float8_e4m3fn_x4
+ALU = mybir.AluOpType
+ACT = mybir.ActivationFunctionType
+X_AXIS = mybir.AxisListType.X
+
+P = 128
+PACK = 4
+HEADS = 2
+ROWS = 16
+COLS = 256
+POSITIONS = ROWS * COLS
+KEYS = ROWS + COLS
+HALVES = COLS // P
+NEG_INF = -1.0e9
+
+CHUNK_ROWS = 4
+CHUNK = CHUNK_ROWS * COLS
+RUN = 4
+VECTOR_SHARE = 3 * CHUNK // 8
+
+OCT = 8
+OCTETS = COLS // OCT
+BANK_OCTETS = 4
+
+BATCH_ROWS = 4
+BATCH = BATCH_ROWS * HALVES
+SCALAR_EVERY = 3
+
+FLOPS = 2 * HEADS * POSITIONS * KEYS * P * PACK
+
+
+def tile_multiheadcrisscrossattention_pa_t_kernel(tc, q, k, out):
+    nc = tc.nc
+    with (
+        tc.tile_pool(name="keep", bufs=1) as keep,
+        tc.tile_pool(name="raw_pool", bufs=4) as raw_pool,
+        tc.tile_pool(name="grouped_pool", bufs=3) as grouped_pool,
+        tc.tile_pool(name="att_pool", bufs=3) as att_pool,
+        tc.tile_pool(name="stat_pool", bufs=3) as stat_pool,
+        tc.psum_pool(name="col_psum", bufs=2) as col_psum,
+        tc.psum_pool(name="row_psum", bufs=6) as row_psum,
+    ):
+        row_codes = {}
+        row_scales = {}
+        for n in range(HEADS):
+            for name in ("q", "k"):
+                row_codes[name, n] = keep.tile(
+                    [P, POSITIONS], U32, align_bytes=64, name="row_codes_%s%d" % (name, n)
+                )
+                row_scales[name, n] = keep.tile(
+                    [P, POSITIONS], U8, align_bytes=64, name="row_scales_%s%d" % (name, n)
+                )
+                nc.vector.memset(row_scales[name, n][:].bitcast(I32), 0)
+        col_codes = {}
+        col_scales = {}
+        for name in ("q", "k"):
+            col_codes[name] = keep.tile(
+                [P, POSITIONS], U32, align_bytes=64, name="col_codes_%s" % name
+            )
+            col_scales[name] = keep.tile(
+                [P, POSITIONS], U8, align_bytes=64, name="col_scales_%s" % name
+            )
+
+        col_energy = {}
+        neg_col_max = {}
+
+        for n in range(HEADS):
+            for name, source in (("q", q), ("k", k)):
+                channels = source[0, n].rearrange("(p t) h w -> p t (h w)", t=PACK)
+                for c in range(ROWS // CHUNK_ROWS):
+                    chunk = slice(c * CHUNK, (c + 1) * CHUNK)
+                    raw = raw_pool.tile([P, PACK, CHUNK], BF16)
+                    nc.sync.dma_start(out=raw[:], in_=channels[:, :, chunk])
+
+                    grouped = grouped_pool.tile([P, CHUNK, PACK], BF16, align_bytes=64)
+                    for copy, share in (
+                        (nc.vector.tensor_copy, slice(0, VECTOR_SHARE)),
+                        (nc.scalar.copy, slice(VECTOR_SHARE, CHUNK)),
+                    ):
+                        copy(
+                            out=grouped[:, share, :].rearrange("p (c i) t -> p c t i", i=RUN),
+                            in_=raw[:, :, share].rearrange("p t (c i) -> p c t i", i=RUN),
+                        )
+                    nc.vector.quantize_mx(
+                        out=row_codes[name, n][:, chunk].bitcast(FP8X4),
+                        scales=row_scales[name, n][:, chunk],
+                        in_=grouped[:].rearrange("p c t -> p (c t)"),
+                    )
+
+                    chunk_rows = slice(c * CHUNK_ROWS, (c + 1) * CHUNK_ROWS)
+                    nc.vector.tensor_copy(
+                        out=col_codes[name][:]
+                        .bitcast(I32)
+                        .rearrange("p (g h u) -> p g h u", h=ROWS, u=OCT)[:, :, chunk_rows, :],
+                        in_=row_codes[name, n][:, chunk]
+                        .bitcast(I32)
+                        .rearrange("p (h g u) -> p g h u", g=OCTETS, u=OCT),
+                    )
+                    nc.vector.tensor_copy(
+                        out=col_scales[name][:]
+                        .bitcast(I32)
+                        .rearrange("p (g h e) -> p g h e", h=ROWS, e=OCT // 4)[:, :, chunk_rows, :],
+                        in_=row_scales[name, n][:, chunk]
+                        .bitcast(I32)
+                        .rearrange("p (h g e) -> p g h e", g=OCTETS, e=OCT // 4),
+                    )
+
+            products = keep.tile([P, OCTETS, OCT, ROWS], F32, name="products")
+            for b in range(OCTETS // BANK_OCTETS):
+                col_bank = col_psum.tile([P, BANK_OCTETS, P], F32)
+                for i in range(BANK_OCTETS):
+                    g = b * BANK_OCTETS + i
+                    octet = slice(g * P, (g + 1) * P)
+                    nc.tensor.matmul_mx(
+                        out=col_bank[:, i, :],
+                        lhsT=col_codes["q"][:, octet].bitcast(FP8X4),
+                        lhsT_scale=col_scales["q"][:, octet],
+                        rhs=col_codes["k"][:, octet].bitcast(FP8X4),
+                        rhs_scale=col_scales["k"][:, octet],
+                        start=True,
+                        stop=True,
+                    )
+                nc.scalar.copy(
+                    out=products[:, b * BANK_OCTETS : (b + 1) * BANK_OCTETS, :, :],
+                    in_=col_bank[:].rearrange("p g (j u) -> p g u j", u=OCT),
+                )
+            by_u = out[0, n].rearrange("h (g u) c -> u h g c", u=OCT)
+            for u in range(OCT):
+                nc.gpsimd.dma_start(out=by_u[u, :, :, 0:ROWS], in_=products[u:P:OCT, :, u, :])
+            col_energy[n] = keep.tile(
+                [P, ROWS * HALVES, ROWS], F32, name="col_energy_%d" % n
+            )
+            nc.gpsimd.dma_start(
+                out=col_energy[n][:],
+                in_=out[0, n].rearrange("h (s w) c -> w (h s) c", s=HALVES)[:, :, 0:ROWS],
+            )
+            for h in range(ROWS):
+                nc.gpsimd.memset(col_energy[n][:, h * HALVES : (h + 1) * HALVES, h : h + 1], NEG_INF)
+            neg_col_max[n] = keep.tile([P, ROWS * HALVES], F32, name="neg_col_max_%d" % n)
+            nc.vector.tensor_reduce(
+                out=neg_col_max[n][:], in_=col_energy[n][:], axis=X_AXIS, op=ALU.max, negate=True
+            )
+
+        for n in range(HEADS):
+            for b in range(ROWS // BATCH_ROWS):
+                tiles = slice(b * BATCH, (b + 1) * BATCH)
+                att = att_pool.tile([P, BATCH, KEYS], F32)
+                neg_row_max = stat_pool.tile([P, BATCH], F32)
+                row_banks = []
+                for i in range(BATCH_ROWS):
+                    h = b * BATCH_ROWS + i
+                    row_bank = row_psum.tile([P, HALVES, COLS], F32)
+                    for s in range(HALVES):
+                        queries = slice(h * COLS + s * P, h * COLS + (s + 1) * P)
+                        keys = slice(h * COLS, (h + 1) * COLS)
+                        nc.tensor.matmul_mx(
+                            out=row_bank[:, s, :],
+                            lhsT=row_codes["q", n][:, queries].bitcast(FP8X4),
+                            lhsT_scale=row_scales["q", n][:, queries],
+                            rhs=row_codes["k", n][:, keys].bitcast(FP8X4),
+                            rhs_scale=row_scales["k", n][:, keys],
+                            start=True,
+                            stop=True,
+                        )
+                    nc.vector.tensor_reduce(
+                        out=neg_row_max[:, i * HALVES : (i + 1) * HALVES],
+                        in_=row_bank[:],
+                        axis=X_AXIS,
+                        op=ALU.max,
+                        negate=True,
+                    )
+                    row_banks.append(row_bank)
+
+                neg_max = stat_pool.tile([P, BATCH], F32)
+                nc.vector.tensor_tensor(
+                    out=neg_max[:], in0=neg_row_max[:], in1=neg_col_max[n][:, tiles], op=ALU.min
+                )
+
+                shifted = stat_pool.tile([P, BATCH, ROWS], F32)
+                nc.vector.tensor_tensor(
+                    out=shifted[:],
+                    in0=col_energy[n][:, tiles, :],
+                    in1=neg_max[:].unsqueeze(2).to_broadcast([P, BATCH, ROWS]),
+                    op=ALU.add,
+                )
+                nc.scalar.activation(out=att[:, :, 0:ROWS], in_=shifted[:], func=ACT.Exp)
+                col_sum = stat_pool.tile([P, BATCH], F32)
+                nc.vector.tensor_reduce(
+                    out=col_sum[:], in_=att[:, :, 0:ROWS], axis=X_AXIS, op=ALU.add
+                )
+
+                row_sum = stat_pool.tile([P, BATCH], F32)
+                for t in range(BATCH):
+                    nc.scalar.activation(
+                        out=att[:, t, ROWS:KEYS],
+                        in_=row_banks[t // HALVES][:, t % HALVES, :],
+                        func=ACT.Exp,
+                        bias=neg_max[:, t : t + 1],
+                        scale=1.0,
+                        accum_out=row_sum[:, t : t + 1],
+                    )
+
+                inv_sum = stat_pool.tile([P, BATCH], F32)
+                nc.vector.tensor_tensor(out=inv_sum[:], in0=row_sum[:], in1=col_sum[:], op=ALU.add)
+                nc.vector.reciprocal(out=inv_sum[:], in_=inv_sum[:])
+                for t in range(BATCH):
+                    if t % SCALAR_EVERY == 0:
+                        nc.scalar.activation(
+                            out=att[:, t, :], in_=att[:, t, :], func=ACT.Copy, scale=inv_sum[:, t : t + 1]
+                        )
+                    else:
+                        nc.vector.tensor_scalar(
+                            out=att[:, t, :],
+                            in0=att[:, t, :],
+                            scalar1=inv_sum[:, t : t + 1],
+                            scalar2=None,
+                            op0=ALU.mult,
+                        )
+                for i in range(BATCH_ROWS):
+                    nc.sync.dma_start(
+                        out=out[0, n, b * BATCH_ROWS + i].rearrange("(s w) c -> w s c", s=HALVES),
+                        in_=att[:, i * HALVES : (i + 1) * HALVES, :],
+                    )

@@ -22,12 +22,14 @@ NEG_INF = -1.0e9
 
 CHUNK_ROWS = 4
 CHUNK = CHUNK_ROWS * COLS
+RAW_BUFS = 4
 RUN = 4
 VECTOR_SHARE = 3 * CHUNK // 8
 
 OCT = 8
 OCTETS = COLS // OCT
 BANK_OCTETS = 4
+PSUM_BANKS = 8
 
 BATCH_ROWS = 4
 BATCH = BATCH_ROWS * HALVES
@@ -40,13 +42,17 @@ def tile_multiheadcrisscrossattention_pa_t_kernel(tc, q, k, out):
     nc = tc.nc
     with (
         tc.tile_pool(name="keep", bufs=1) as keep,
-        tc.tile_pool(name="raw_pool", bufs=4) as raw_pool,
+        tc.tile_pool(name="raw_pool", bufs=RAW_BUFS) as raw_pool,
         tc.tile_pool(name="grouped_pool", bufs=3) as grouped_pool,
         tc.tile_pool(name="att_pool", bufs=3) as att_pool,
         tc.tile_pool(name="stat_pool", bufs=3) as stat_pool,
-        tc.psum_pool(name="col_psum", bufs=2) as col_psum,
-        tc.psum_pool(name="row_psum", bufs=6) as row_psum,
+        tc.psum_pool(name="psum", bufs=PSUM_BANKS) as psum,
+        tc.manual_schedule(),
     ):
+        warm = keep.tile([P, 1], F32, name="warm")
+        nc.vector.memset(warm[:], 0.0)
+        nc.scalar.activation(out=warm[:], in_=warm[:], func=ACT.Exp)
+
         row_codes = {}
         row_scales = {}
         for n in range(HEADS):
@@ -68,53 +74,62 @@ def tile_multiheadcrisscrossattention_pa_t_kernel(tc, q, k, out):
                 [P, POSITIONS], U8, align_bytes=64, name="col_scales_%s" % name
             )
 
-        col_energy = {}
-        neg_col_max = {}
+        chunks = [
+            (n, name, source, c)
+            for n in range(HEADS)
+            for name, source in (("q", q), ("k", k))
+            for c in range(ROWS // CHUNK_ROWS)
+        ]
 
-        for n in range(HEADS):
-            for name, source in (("q", q), ("k", k)):
-                channels = source[0, n].rearrange("(p t) h w -> p t (h w)", t=PACK)
-                for c in range(ROWS // CHUNK_ROWS):
-                    chunk = slice(c * CHUNK, (c + 1) * CHUNK)
-                    raw = raw_pool.tile([P, PACK, CHUNK], BF16)
-                    nc.sync.dma_start(out=raw[:], in_=channels[:, :, chunk])
+        def load(chunk):
+            n, name, source, c = chunk
+            channels = source[0, n].rearrange("(p t) h w -> p t (h w)", t=PACK)
+            raw = raw_pool.tile([P, PACK, CHUNK], BF16)
+            nc.sync.dma_start(out=raw[:], in_=channels[:, :, c * CHUNK : (c + 1) * CHUNK])
+            return raw
 
-                    grouped = grouped_pool.tile([P, CHUNK, PACK], BF16, align_bytes=64)
-                    for copy, share in (
-                        (nc.vector.tensor_copy, slice(0, VECTOR_SHARE)),
-                        (nc.scalar.copy, slice(VECTOR_SHARE, CHUNK)),
-                    ):
-                        copy(
-                            out=grouped[:, share, :].rearrange("p (c i) t -> p c t i", i=RUN),
-                            in_=raw[:, :, share].rearrange("p t (c i) -> p c t i", i=RUN),
-                        )
-                    nc.vector.quantize_mx(
-                        out=row_codes[name, n][:, chunk].bitcast(FP8X4),
-                        scales=row_scales[name, n][:, chunk],
-                        in_=grouped[:].rearrange("p c t -> p (c t)"),
-                    )
+        def regroup(raw):
+            grouped = grouped_pool.tile([P, CHUNK, PACK], BF16, align_bytes=64)
+            for copy, share in (
+                (nc.vector.tensor_copy, slice(0, VECTOR_SHARE)),
+                (nc.scalar.copy, slice(VECTOR_SHARE, CHUNK)),
+            ):
+                copy(
+                    out=grouped[:, share, :].rearrange("p (c i) t -> p c t i", i=RUN),
+                    in_=raw[:, :, share].rearrange("p t (c i) -> p c t i", i=RUN),
+                )
+            return grouped
 
-                    chunk_rows = slice(c * CHUNK_ROWS, (c + 1) * CHUNK_ROWS)
-                    nc.vector.tensor_copy(
-                        out=col_codes[name][:]
-                        .bitcast(I32)
-                        .rearrange("p (g h u) -> p g h u", h=ROWS, u=OCT)[:, :, chunk_rows, :],
-                        in_=row_codes[name, n][:, chunk]
-                        .bitcast(I32)
-                        .rearrange("p (h g u) -> p g h u", g=OCTETS, u=OCT),
-                    )
-                    nc.vector.tensor_copy(
-                        out=col_scales[name][:]
-                        .bitcast(I32)
-                        .rearrange("p (g h e) -> p g h e", h=ROWS, e=OCT // 4)[:, :, chunk_rows, :],
-                        in_=row_scales[name, n][:, chunk]
-                        .bitcast(I32)
-                        .rearrange("p (h g e) -> p g h e", g=OCTETS, e=OCT // 4),
-                    )
+        def quantise_and_move(chunk, grouped):
+            n, name, source, c = chunk
+            positions = slice(c * CHUNK, (c + 1) * CHUNK)
+            nc.vector.quantize_mx(
+                out=row_codes[name, n][:, positions].bitcast(FP8X4),
+                scales=row_scales[name, n][:, positions],
+                in_=grouped[:].rearrange("p c t -> p (c t)"),
+            )
+            chunk_rows = slice(c * CHUNK_ROWS, (c + 1) * CHUNK_ROWS)
+            nc.vector.tensor_copy(
+                out=col_codes[name][:]
+                .bitcast(I32)
+                .rearrange("p (g h u) -> p g h u", h=ROWS, u=OCT)[:, :, chunk_rows, :],
+                in_=row_codes[name, n][:, positions]
+                .bitcast(I32)
+                .rearrange("p (h g u) -> p g h u", g=OCTETS, u=OCT),
+            )
+            nc.vector.tensor_copy(
+                out=col_scales[name][:]
+                .bitcast(I32)
+                .rearrange("p (g h e) -> p g h e", h=ROWS, e=OCT // 4)[:, :, chunk_rows, :],
+                in_=row_scales[name, n][:, positions]
+                .bitcast(I32)
+                .rearrange("p (h g e) -> p g h e", g=OCTETS, e=OCT // 4),
+            )
 
+        def column_products(n):
             products = keep.tile([P, OCTETS, OCT, ROWS], F32, name="products")
             for b in range(OCTETS // BANK_OCTETS):
-                col_bank = col_psum.tile([P, BANK_OCTETS, P], F32)
+                col_bank = psum.tile([P, BANK_OCTETS, P], F32, tag="bank")
                 for i in range(BANK_OCTETS):
                     g = b * BANK_OCTETS + i
                     octet = slice(g * P, (g + 1) * P)
@@ -133,98 +148,136 @@ def tile_multiheadcrisscrossattention_pa_t_kernel(tc, q, k, out):
                 )
             by_u = out[0, n].rearrange("h (g u) c -> u h g c", u=OCT)
             for u in range(OCT):
-                nc.gpsimd.dma_start(out=by_u[u, :, :, 0:ROWS], in_=products[u:P:OCT, :, u, :])
-            col_energy[n] = keep.tile(
-                [P, ROWS * HALVES, ROWS], F32, name="col_energy_%d" % n
-            )
-            nc.gpsimd.dma_start(
+                nc.scalar.dma_start(out=by_u[u, :, :, 0:ROWS], in_=products[u:P:OCT, :, u, :])
+
+        col_energy = {}
+        neg_col_max = {}
+
+        def column_energies_back(n):
+            col_energy[n] = keep.tile([P, ROWS * HALVES, ROWS], F32, name="col_energy_%d" % n)
+            nc.sync.dma_start(
                 out=col_energy[n][:],
                 in_=out[0, n].rearrange("h (s w) c -> w (h s) c", s=HALVES)[:, :, 0:ROWS],
             )
-            for h in range(ROWS):
-                nc.gpsimd.memset(col_energy[n][:, h * HALVES : (h + 1) * HALVES, h : h + 1], NEG_INF)
+
+        def column_mask_and_max(n):
+            flat = col_energy[n][:].rearrange("p t j -> p (t j)")
+            for s in range(HALVES):
+                nc.gpsimd.memset(flat[:, s * ROWS :: HALVES * ROWS + 1], NEG_INF)
             neg_col_max[n] = keep.tile([P, ROWS * HALVES], F32, name="neg_col_max_%d" % n)
             nc.vector.tensor_reduce(
                 out=neg_col_max[n][:], in_=col_energy[n][:], axis=X_AXIS, op=ALU.max, negate=True
             )
 
+        raws = [load(chunk) for chunk in chunks[: RAW_BUFS - 1]]
+        regrouped = None
+        for i in range(len(chunks) + 1):
+            if i + RAW_BUFS - 1 < len(chunks):
+                raws.append(load(chunks[i + RAW_BUFS - 1]))
+            previous = regrouped
+            if i < len(chunks):
+                regrouped = regroup(raws[i])
+            if i > 0:
+                quantise_and_move(chunks[i - 1], previous)
+                if i % (len(chunks) // HEADS) == 0:
+                    column_products(chunks[i - 1][0])
         for n in range(HEADS):
-            for b in range(ROWS // BATCH_ROWS):
-                tiles = slice(b * BATCH, (b + 1) * BATCH)
-                att = att_pool.tile([P, BATCH, KEYS], F32)
-                neg_row_max = stat_pool.tile([P, BATCH], F32)
-                row_banks = []
-                for i in range(BATCH_ROWS):
-                    h = b * BATCH_ROWS + i
-                    row_bank = row_psum.tile([P, HALVES, COLS], F32)
-                    for s in range(HALVES):
-                        queries = slice(h * COLS + s * P, h * COLS + (s + 1) * P)
-                        keys = slice(h * COLS, (h + 1) * COLS)
-                        nc.tensor.matmul_mx(
-                            out=row_bank[:, s, :],
-                            lhsT=row_codes["q", n][:, queries].bitcast(FP8X4),
-                            lhsT_scale=row_scales["q", n][:, queries],
-                            rhs=row_codes["k", n][:, keys].bitcast(FP8X4),
-                            rhs_scale=row_scales["k", n][:, keys],
-                            start=True,
-                            stop=True,
-                        )
-                    nc.vector.tensor_reduce(
-                        out=neg_row_max[:, i * HALVES : (i + 1) * HALVES],
-                        in_=row_bank[:],
-                        axis=X_AXIS,
-                        op=ALU.max,
-                        negate=True,
+            column_energies_back(n)
+
+        batches = [(n, b) for n in range(HEADS) for b in range(ROWS // BATCH_ROWS)]
+        state = {}
+
+        def energies(batch):
+            n, b = batch
+            if b == 0:
+                column_mask_and_max(n)
+            tiles = slice(b * BATCH, (b + 1) * BATCH)
+            neg_row_max = stat_pool.tile([P, BATCH], F32)
+            row_banks = []
+            for i in range(BATCH_ROWS):
+                h = b * BATCH_ROWS + i
+                row_bank = psum.tile([P, HALVES, COLS], F32, tag="bank")
+                for s in range(HALVES):
+                    queries = slice(h * COLS + s * P, h * COLS + (s + 1) * P)
+                    keys = slice(h * COLS, (h + 1) * COLS)
+                    nc.tensor.matmul_mx(
+                        out=row_bank[:, s, :],
+                        lhsT=row_codes["q", n][:, queries].bitcast(FP8X4),
+                        lhsT_scale=row_scales["q", n][:, queries],
+                        rhs=row_codes["k", n][:, keys].bitcast(FP8X4),
+                        rhs_scale=row_scales["k", n][:, keys],
+                        start=True,
+                        stop=True,
                     )
-                    row_banks.append(row_bank)
-
-                neg_max = stat_pool.tile([P, BATCH], F32)
-                nc.vector.tensor_tensor(
-                    out=neg_max[:], in0=neg_row_max[:], in1=neg_col_max[n][:, tiles], op=ALU.min
-                )
-
-                shifted = stat_pool.tile([P, BATCH, ROWS], F32)
-                nc.vector.tensor_tensor(
-                    out=shifted[:],
-                    in0=col_energy[n][:, tiles, :],
-                    in1=neg_max[:].unsqueeze(2).to_broadcast([P, BATCH, ROWS]),
-                    op=ALU.add,
-                )
-                nc.scalar.activation(out=att[:, :, 0:ROWS], in_=shifted[:], func=ACT.Exp)
-                col_sum = stat_pool.tile([P, BATCH], F32)
                 nc.vector.tensor_reduce(
-                    out=col_sum[:], in_=att[:, :, 0:ROWS], axis=X_AXIS, op=ALU.add
+                    out=neg_row_max[:, i * HALVES : (i + 1) * HALVES],
+                    in_=row_bank[:],
+                    axis=X_AXIS,
+                    op=ALU.max,
+                    negate=True,
+                )
+                row_banks.append(row_bank)
+            neg_max = stat_pool.tile([P, BATCH], F32)
+            nc.vector.tensor_tensor(
+                out=neg_max[:], in0=neg_row_max[:], in1=neg_col_max[n][:, tiles], op=ALU.min
+            )
+            shifted = stat_pool.tile([P, BATCH, ROWS], F32)
+            nc.vector.tensor_tensor(
+                out=shifted[:],
+                in0=col_energy[n][:, tiles, :],
+                in1=neg_max[:].unsqueeze(2).to_broadcast([P, BATCH, ROWS]),
+                op=ALU.add,
+            )
+            state[batch] = (row_banks, neg_max, shifted)
+
+        def exponentials(batch):
+            row_banks, neg_max, shifted = state[batch]
+            att = att_pool.tile([P, BATCH, KEYS], F32)
+            nc.scalar.activation(out=att[:, :, 0:ROWS], in_=shifted[:], func=ACT.Exp)
+            row_sum = stat_pool.tile([P, BATCH], F32)
+            for t in range(BATCH):
+                nc.scalar.activation(
+                    out=att[:, t, ROWS:KEYS],
+                    in_=row_banks[t // HALVES][:, t % HALVES, :],
+                    func=ACT.Exp,
+                    bias=neg_max[:, t : t + 1],
+                    scale=1.0,
+                    accum_out=row_sum[:, t : t + 1],
+                )
+            state[batch] = (att, row_sum)
+
+        def scale_and_store(batch):
+            n, b = batch
+            att, row_sum = state[batch]
+            inv_sum = stat_pool.tile([P, BATCH], F32)
+            nc.vector.tensor_reduce(out=inv_sum[:], in_=att[:, :, 0:ROWS], axis=X_AXIS, op=ALU.add)
+            nc.vector.tensor_tensor(out=inv_sum[:], in0=inv_sum[:], in1=row_sum[:], op=ALU.add)
+            nc.vector.reciprocal(out=inv_sum[:], in_=inv_sum[:])
+            for t in range(BATCH):
+                if t % SCALAR_EVERY == 0:
+                    nc.scalar.activation(
+                        out=att[:, t, :], in_=att[:, t, :], func=ACT.Copy, scale=inv_sum[:, t : t + 1]
+                    )
+                else:
+                    nc.vector.tensor_scalar(
+                        out=att[:, t, :],
+                        in0=att[:, t, :],
+                        scalar1=inv_sum[:, t : t + 1],
+                        scalar2=None,
+                        op0=ALU.mult,
+                    )
+            for i in range(BATCH_ROWS):
+                nc.sync.dma_start(
+                    out=out[0, n, b * BATCH_ROWS + i].rearrange("(s w) c -> w s c", s=HALVES),
+                    in_=att[:, i * HALVES : (i + 1) * HALVES, :],
                 )
 
-                row_sum = stat_pool.tile([P, BATCH], F32)
-                for t in range(BATCH):
-                    nc.scalar.activation(
-                        out=att[:, t, ROWS:KEYS],
-                        in_=row_banks[t // HALVES][:, t % HALVES, :],
-                        func=ACT.Exp,
-                        bias=neg_max[:, t : t + 1],
-                        scale=1.0,
-                        accum_out=row_sum[:, t : t + 1],
-                    )
-
-                inv_sum = stat_pool.tile([P, BATCH], F32)
-                nc.vector.tensor_tensor(out=inv_sum[:], in0=row_sum[:], in1=col_sum[:], op=ALU.add)
-                nc.vector.reciprocal(out=inv_sum[:], in_=inv_sum[:])
-                for t in range(BATCH):
-                    if t % SCALAR_EVERY == 0:
-                        nc.scalar.activation(
-                            out=att[:, t, :], in_=att[:, t, :], func=ACT.Copy, scale=inv_sum[:, t : t + 1]
-                        )
-                    else:
-                        nc.vector.tensor_scalar(
-                            out=att[:, t, :],
-                            in0=att[:, t, :],
-                            scalar1=inv_sum[:, t : t + 1],
-                            scalar2=None,
-                            op0=ALU.mult,
-                        )
-                for i in range(BATCH_ROWS):
-                    nc.sync.dma_start(
-                        out=out[0, n, b * BATCH_ROWS + i].rearrange("(s w) c -> w s c", s=HALVES),
-                        in_=att[:, i * HALVES : (i + 1) * HALVES, :],
-                    )
+        energies(batches[0])
+        exponentials(batches[0])
+        energies(batches[1])
+        for i in range(len(batches)):
+            if i + 1 < len(batches):
+                exponentials(batches[i + 1])
+            scale_and_store(batches[i])
+            if i + 2 < len(batches):
+                energies(batches[i + 2])

@@ -22,7 +22,7 @@ NEG_INF = -1.0e9
 
 CHUNK_ROWS = 4
 CHUNK = CHUNK_ROWS * COLS
-RAW_BUFS = 4
+RAW_BUFS = 5
 RUN = 4
 VECTOR_SHARE = 3 * CHUNK // 8
 
@@ -34,6 +34,7 @@ PSUM_BANKS = 8
 BATCH_ROWS = 4
 BATCH = BATCH_ROWS * HALVES
 SCALAR_EVERY = 3
+ATT_BUFS = 6
 
 FLOPS = 2 * HEADS * POSITIONS * KEYS * P * PACK
 
@@ -42,12 +43,8 @@ def tile_multiheadcrisscrossattention_pa_t_kernel(tc, q, k, out):
     nc = tc.nc
     with (
         tc.tile_pool(name="keep", bufs=1) as keep,
-        tc.tile_pool(name="raw_pool", bufs=RAW_BUFS) as raw_pool,
-        tc.tile_pool(name="grouped_pool", bufs=3) as grouped_pool,
-        tc.tile_pool(name="att_pool", bufs=3) as att_pool,
-        tc.tile_pool(name="stat_pool", bufs=3) as stat_pool,
+        tc.tile_pool(name="stat_pool", bufs=4) as stat_pool,
         tc.psum_pool(name="psum", bufs=PSUM_BANKS) as psum,
-        tc.manual_schedule(),
     ):
         warm = keep.tile([P, 1], F32, name="warm")
         nc.vector.memset(warm[:], 0.0)
@@ -64,94 +61,8 @@ def tile_multiheadcrisscrossattention_pa_t_kernel(tc, q, k, out):
                     [P, POSITIONS], U8, align_bytes=64, name="row_scales_%s%d" % (name, n)
                 )
                 nc.vector.memset(row_scales[name, n][:].bitcast(I32), 0)
-        col_codes = {}
-        col_scales = {}
-        for name in ("q", "k"):
-            col_codes[name] = keep.tile(
-                [P, POSITIONS], U32, align_bytes=64, name="col_codes_%s" % name
-            )
-            col_scales[name] = keep.tile(
-                [P, POSITIONS], U8, align_bytes=64, name="col_scales_%s" % name
-            )
-
-        chunks = [
-            (n, name, source, c)
-            for n in range(HEADS)
-            for name, source in (("q", q), ("k", k))
-            for c in range(ROWS // CHUNK_ROWS)
-        ]
-
-        def load(chunk):
-            n, name, source, c = chunk
-            channels = source[0, n].rearrange("(p t) h w -> p t (h w)", t=PACK)
-            raw = raw_pool.tile([P, PACK, CHUNK], BF16)
-            nc.sync.dma_start(out=raw[:], in_=channels[:, :, c * CHUNK : (c + 1) * CHUNK])
-            return raw
-
-        def regroup(raw):
-            grouped = grouped_pool.tile([P, CHUNK, PACK], BF16, align_bytes=64)
-            for copy, share in (
-                (nc.vector.tensor_copy, slice(0, VECTOR_SHARE)),
-                (nc.scalar.copy, slice(VECTOR_SHARE, CHUNK)),
-            ):
-                copy(
-                    out=grouped[:, share, :].rearrange("p (c i) t -> p c t i", i=RUN),
-                    in_=raw[:, :, share].rearrange("p t (c i) -> p c t i", i=RUN),
-                )
-            return grouped
-
-        def quantise_and_move(chunk, grouped):
-            n, name, source, c = chunk
-            positions = slice(c * CHUNK, (c + 1) * CHUNK)
-            nc.vector.quantize_mx(
-                out=row_codes[name, n][:, positions].bitcast(FP8X4),
-                scales=row_scales[name, n][:, positions],
-                in_=grouped[:].rearrange("p c t -> p (c t)"),
-            )
-            chunk_rows = slice(c * CHUNK_ROWS, (c + 1) * CHUNK_ROWS)
-            nc.vector.tensor_copy(
-                out=col_codes[name][:]
-                .bitcast(I32)
-                .rearrange("p (g h u) -> p g h u", h=ROWS, u=OCT)[:, :, chunk_rows, :],
-                in_=row_codes[name, n][:, positions]
-                .bitcast(I32)
-                .rearrange("p (h g u) -> p g h u", g=OCTETS, u=OCT),
-            )
-            nc.vector.tensor_copy(
-                out=col_scales[name][:]
-                .bitcast(I32)
-                .rearrange("p (g h e) -> p g h e", h=ROWS, e=OCT // 4)[:, :, chunk_rows, :],
-                in_=row_scales[name, n][:, positions]
-                .bitcast(I32)
-                .rearrange("p (h g e) -> p g h e", g=OCTETS, e=OCT // 4),
-            )
-
-        def column_products(n):
-            products = keep.tile([P, OCTETS, OCT, ROWS], F32, name="products")
-            for b in range(OCTETS // BANK_OCTETS):
-                col_bank = psum.tile([P, BANK_OCTETS, P], F32, tag="bank")
-                for i in range(BANK_OCTETS):
-                    g = b * BANK_OCTETS + i
-                    octet = slice(g * P, (g + 1) * P)
-                    nc.tensor.matmul_mx(
-                        out=col_bank[:, i, :],
-                        lhsT=col_codes["q"][:, octet].bitcast(FP8X4),
-                        lhsT_scale=col_scales["q"][:, octet],
-                        rhs=col_codes["k"][:, octet].bitcast(FP8X4),
-                        rhs_scale=col_scales["k"][:, octet],
-                        start=True,
-                        stop=True,
-                    )
-                nc.scalar.copy(
-                    out=products[:, b * BANK_OCTETS : (b + 1) * BANK_OCTETS, :, :],
-                    in_=col_bank[:].rearrange("p g (j u) -> p g u j", u=OCT),
-                )
-            by_u = out[0, n].rearrange("h (g u) c -> u h g c", u=OCT)
-            for u in range(OCT):
-                nc.scalar.dma_start(out=by_u[u, :, :, 0:ROWS], in_=products[u:P:OCT, :, u, :])
 
         col_energy = {}
-        neg_col_max = {}
 
         def column_energies_back(n):
             col_energy[n] = keep.tile([P, ROWS * HALVES, ROWS], F32, name="col_energy_%d" % n)
@@ -160,124 +71,227 @@ def tile_multiheadcrisscrossattention_pa_t_kernel(tc, q, k, out):
                 in_=out[0, n].rearrange("h (s w) c -> w (h s) c", s=HALVES)[:, :, 0:ROWS],
             )
 
-        def column_mask_and_max(n):
-            flat = col_energy[n][:].rearrange("p t j -> p (t j)")
-            for s in range(HALVES):
-                nc.gpsimd.memset(flat[:, s * ROWS :: HALVES * ROWS + 1], NEG_INF)
-            neg_col_max[n] = keep.tile([P, ROWS * HALVES], F32, name="neg_col_max_%d" % n)
-            nc.vector.tensor_reduce(
-                out=neg_col_max[n][:], in_=col_energy[n][:], axis=X_AXIS, op=ALU.max, negate=True
-            )
+        with (
+            tc.tile_pool(name="raw_pool", bufs=RAW_BUFS) as raw_pool,
+            tc.tile_pool(name="grouped_pool", bufs=4) as grouped_pool,
+            tc.tile_pool(name="col_pool", bufs=1) as col_pool,
+        ):
+            col_codes = {}
+            col_scales = {}
+            for name in ("q", "k"):
+                col_codes[name] = col_pool.tile(
+                    [P, POSITIONS], U32, align_bytes=64, name="col_codes_%s" % name
+                )
+                col_scales[name] = col_pool.tile(
+                    [P, POSITIONS], U8, align_bytes=64, name="col_scales_%s" % name
+                )
 
-        raws = [load(chunk) for chunk in chunks[: RAW_BUFS - 1]]
-        regrouped = None
-        for i in range(len(chunks) + 1):
-            if i + RAW_BUFS - 1 < len(chunks):
-                raws.append(load(chunks[i + RAW_BUFS - 1]))
-            previous = regrouped
-            if i < len(chunks):
-                regrouped = regroup(raws[i])
-            if i > 0:
-                quantise_and_move(chunks[i - 1], previous)
-                if i % (len(chunks) // HEADS) == 0:
-                    column_products(chunks[i - 1][0])
-        for n in range(HEADS):
-            column_energies_back(n)
+            chunks = [
+                (n, name, source, c)
+                for n in range(HEADS)
+                for name, source in (("q", q), ("k", k))
+                for c in range(ROWS // CHUNK_ROWS)
+            ]
 
-        batches = [(n, b) for n in range(HEADS) for b in range(ROWS // BATCH_ROWS)]
-        state = {}
+            def load(chunk):
+                n, name, source, c = chunk
+                channels = source[0, n].rearrange("(p t) h w -> p t (h w)", t=PACK)
+                raw = raw_pool.tile([P, PACK, CHUNK], BF16)
+                nc.sync.dma_start(out=raw[:], in_=channels[:, :, c * CHUNK : (c + 1) * CHUNK])
+                return raw
 
-        def energies(batch):
-            n, b = batch
-            if b == 0:
-                column_mask_and_max(n)
-            tiles = slice(b * BATCH, (b + 1) * BATCH)
-            neg_row_max = stat_pool.tile([P, BATCH], F32)
-            row_banks = []
-            for i in range(BATCH_ROWS):
-                h = b * BATCH_ROWS + i
-                row_bank = psum.tile([P, HALVES, COLS], F32, tag="bank")
+            def regroup(raw):
+                grouped = grouped_pool.tile([P, CHUNK, PACK], BF16, align_bytes=64)
+                for copy, share in (
+                    (nc.vector.tensor_copy, slice(0, VECTOR_SHARE)),
+                    (nc.scalar.copy, slice(VECTOR_SHARE, CHUNK)),
+                ):
+                    copy(
+                        out=grouped[:, share, :].rearrange("p (c i) t -> p c t i", i=RUN),
+                        in_=raw[:, :, share].rearrange("p t (c i) -> p c t i", i=RUN),
+                    )
+                return grouped
+
+            def quantise_and_move(chunk, grouped):
+                n, name, source, c = chunk
+                positions = slice(c * CHUNK, (c + 1) * CHUNK)
+                nc.vector.quantize_mx(
+                    out=row_codes[name, n][:, positions].bitcast(FP8X4),
+                    scales=row_scales[name, n][:, positions],
+                    in_=grouped[:].rearrange("p c t -> p (c t)"),
+                )
+                chunk_rows = slice(c * CHUNK_ROWS, (c + 1) * CHUNK_ROWS)
+                nc.vector.tensor_copy(
+                    out=col_codes[name][:]
+                    .bitcast(I32)
+                    .rearrange("p (g h u) -> p g h u", h=ROWS, u=OCT)[:, :, chunk_rows, :],
+                    in_=row_codes[name, n][:, positions]
+                    .bitcast(I32)
+                    .rearrange("p (h g u) -> p g h u", g=OCTETS, u=OCT),
+                )
+                nc.vector.tensor_copy(
+                    out=col_scales[name][:]
+                    .bitcast(I32)
+                    .rearrange("p (g h e) -> p g h e", h=ROWS, e=OCT // 4)[:, :, chunk_rows, :],
+                    in_=row_scales[name, n][:, positions]
+                    .bitcast(I32)
+                    .rearrange("p (h g e) -> p g h e", g=OCTETS, e=OCT // 4),
+                )
+
+            def column_products(n):
+                products = col_pool.tile([P, OCTETS, OCT, ROWS], F32)
+                for b in range(OCTETS // BANK_OCTETS):
+                    col_bank = psum.tile([P, BANK_OCTETS, P], F32, tag="bank")
+                    for i in range(BANK_OCTETS):
+                        g = b * BANK_OCTETS + i
+                        octet = slice(g * P, (g + 1) * P)
+                        nc.tensor.matmul_mx(
+                            out=col_bank[:, i, :],
+                            lhsT=col_codes["q"][:, octet].bitcast(FP8X4),
+                            lhsT_scale=col_scales["q"][:, octet],
+                            rhs=col_codes["k"][:, octet].bitcast(FP8X4),
+                            rhs_scale=col_scales["k"][:, octet],
+                            start=True,
+                            stop=True,
+                        )
+                    copy = nc.scalar.copy if b % 2 == 0 else nc.vector.tensor_copy
+                    copy(
+                        out=products[:, b * BANK_OCTETS : (b + 1) * BANK_OCTETS, :, :],
+                        in_=col_bank[:].rearrange("p g (j u) -> p g u j", u=OCT),
+                    )
+                by_u = out[0, n].rearrange("h (g u) c -> u h g c", u=OCT)
+                for u in range(OCT):
+                    nc.sync.dma_start(out=by_u[u, :, :, 0:ROWS], in_=products[u:P:OCT, :, u, :])
+
+            raws = [load(chunk) for chunk in chunks[: RAW_BUFS - 1]]
+            regrouped = None
+            for i in range(len(chunks) + 1):
+                if i + RAW_BUFS - 1 < len(chunks):
+                    raws.append(load(chunks[i + RAW_BUFS - 1]))
+                previous = regrouped
+                if i < len(chunks):
+                    regrouped = regroup(raws[i])
+                if i > 0:
+                    quantise_and_move(chunks[i - 1], previous)
+                    if i % (len(chunks) // HEADS) == 0:
+                        n = chunks[i - 1][0]
+                        if n > 0:
+                            column_energies_back(n - 1)
+                        column_products(n)
+
+        column_energies_back(HEADS - 1)
+
+        with tc.tile_pool(name="att_pool", bufs=ATT_BUFS, reuse_waits="tile") as att_pool:
+            neg_col_max = {}
+
+            def column_mask_and_max(n):
+                flat = col_energy[n][:].rearrange("p t j -> p (t j)")
                 for s in range(HALVES):
-                    queries = slice(h * COLS + s * P, h * COLS + (s + 1) * P)
-                    keys = slice(h * COLS, (h + 1) * COLS)
-                    nc.tensor.matmul_mx(
-                        out=row_bank[:, s, :],
-                        lhsT=row_codes["q", n][:, queries].bitcast(FP8X4),
-                        lhsT_scale=row_scales["q", n][:, queries],
-                        rhs=row_codes["k", n][:, keys].bitcast(FP8X4),
-                        rhs_scale=row_scales["k", n][:, keys],
-                        start=True,
-                        stop=True,
-                    )
+                    nc.gpsimd.memset(flat[:, s * ROWS :: HALVES * ROWS + 1], NEG_INF)
+                neg_col_max[n] = keep.tile([P, ROWS * HALVES], F32, name="neg_col_max_%d" % n)
                 nc.vector.tensor_reduce(
-                    out=neg_row_max[:, i * HALVES : (i + 1) * HALVES],
-                    in_=row_bank[:],
-                    axis=X_AXIS,
-                    op=ALU.max,
-                    negate=True,
+                    out=neg_col_max[n][:], in_=col_energy[n][:], axis=X_AXIS, op=ALU.max, negate=True
                 )
-                row_banks.append(row_bank)
-            neg_max = stat_pool.tile([P, BATCH], F32)
-            nc.vector.tensor_tensor(
-                out=neg_max[:], in0=neg_row_max[:], in1=neg_col_max[n][:, tiles], op=ALU.min
-            )
-            shifted = stat_pool.tile([P, BATCH, ROWS], F32)
-            nc.vector.tensor_tensor(
-                out=shifted[:],
-                in0=col_energy[n][:, tiles, :],
-                in1=neg_max[:].unsqueeze(2).to_broadcast([P, BATCH, ROWS]),
-                op=ALU.add,
-            )
-            state[batch] = (row_banks, neg_max, shifted)
 
-        def exponentials(batch):
-            row_banks, neg_max, shifted = state[batch]
-            att = att_pool.tile([P, BATCH, KEYS], F32)
-            nc.scalar.activation(out=att[:, :, 0:ROWS], in_=shifted[:], func=ACT.Exp)
-            row_sum = stat_pool.tile([P, BATCH], F32)
-            for t in range(BATCH):
-                nc.scalar.activation(
-                    out=att[:, t, ROWS:KEYS],
-                    in_=row_banks[t // HALVES][:, t % HALVES, :],
-                    func=ACT.Exp,
-                    bias=neg_max[:, t : t + 1],
-                    scale=1.0,
-                    accum_out=row_sum[:, t : t + 1],
+            batches = [(n, b) for n in range(HEADS) for b in range(ROWS // BATCH_ROWS)]
+            state = {}
+
+            def energies(batch):
+                n, b = batch
+                if b == 0:
+                    column_mask_and_max(n)
+                tiles = slice(b * BATCH, (b + 1) * BATCH)
+                neg_row_max = stat_pool.tile([P, BATCH], F32)
+                row_banks = []
+                for i in range(BATCH_ROWS):
+                    h = b * BATCH_ROWS + i
+                    row_bank = psum.tile([P, HALVES, COLS], F32, tag="bank")
+                    for s in range(HALVES):
+                        queries = slice(h * COLS + s * P, h * COLS + (s + 1) * P)
+                        keys = slice(h * COLS, (h + 1) * COLS)
+                        nc.tensor.matmul_mx(
+                            out=row_bank[:, s, :],
+                            lhsT=row_codes["q", n][:, queries].bitcast(FP8X4),
+                            lhsT_scale=row_scales["q", n][:, queries],
+                            rhs=row_codes["k", n][:, keys].bitcast(FP8X4),
+                            rhs_scale=row_scales["k", n][:, keys],
+                            start=True,
+                            stop=True,
+                        )
+                    nc.vector.tensor_reduce(
+                        out=neg_row_max[:, i * HALVES : (i + 1) * HALVES],
+                        in_=row_bank[:],
+                        axis=X_AXIS,
+                        op=ALU.max,
+                        negate=True,
+                    )
+                    row_banks.append(row_bank)
+                neg_max = stat_pool.tile([P, BATCH], F32)
+                nc.vector.tensor_tensor(
+                    out=neg_max[:], in0=neg_row_max[:], in1=neg_col_max[n][:, tiles], op=ALU.min
                 )
-            state[batch] = (att, row_sum)
+                shifted = stat_pool.tile([P, BATCH, ROWS], F32)
+                nc.vector.tensor_tensor(
+                    out=shifted[:],
+                    in0=col_energy[n][:, tiles, :],
+                    in1=neg_max[:].unsqueeze(2).to_broadcast([P, BATCH, ROWS]),
+                    op=ALU.add,
+                )
+                state[batch] = (row_banks, neg_max, shifted)
 
-        def scale_and_store(batch):
-            n, b = batch
-            att, row_sum = state[batch]
-            inv_sum = stat_pool.tile([P, BATCH], F32)
-            nc.vector.tensor_reduce(out=inv_sum[:], in_=att[:, :, 0:ROWS], axis=X_AXIS, op=ALU.add)
-            nc.vector.tensor_tensor(out=inv_sum[:], in0=inv_sum[:], in1=row_sum[:], op=ALU.add)
-            nc.vector.reciprocal(out=inv_sum[:], in_=inv_sum[:])
-            for t in range(BATCH):
-                if t % SCALAR_EVERY == 0:
+            def exponentials(batch):
+                row_banks, neg_max, shifted = state[batch]
+                att = att_pool.tile([P, BATCH, KEYS], F32)
+                nc.scalar.activation(out=att[:, :, 0:ROWS], in_=shifted[:], func=ACT.Exp)
+                row_sum = stat_pool.tile([P, BATCH], F32)
+                for t in range(BATCH):
                     nc.scalar.activation(
-                        out=att[:, t, :], in_=att[:, t, :], func=ACT.Copy, scale=inv_sum[:, t : t + 1]
+                        out=att[:, t, ROWS:KEYS],
+                        in_=row_banks[t // HALVES][:, t % HALVES, :],
+                        func=ACT.Exp,
+                        bias=neg_max[:, t : t + 1],
+                        scale=1.0,
+                        accum_out=row_sum[:, t : t + 1],
                     )
-                else:
-                    nc.vector.tensor_scalar(
-                        out=att[:, t, :],
-                        in0=att[:, t, :],
-                        scalar1=inv_sum[:, t : t + 1],
-                        scalar2=None,
-                        op0=ALU.mult,
-                    )
-            for i in range(BATCH_ROWS):
-                nc.sync.dma_start(
-                    out=out[0, n, b * BATCH_ROWS + i].rearrange("(s w) c -> w s c", s=HALVES),
-                    in_=att[:, i * HALVES : (i + 1) * HALVES, :],
-                )
+                state[batch] = (att, row_sum)
 
-        energies(batches[0])
-        exponentials(batches[0])
-        energies(batches[1])
-        for i in range(len(batches)):
-            if i + 1 < len(batches):
-                exponentials(batches[i + 1])
-            scale_and_store(batches[i])
-            if i + 2 < len(batches):
-                energies(batches[i + 2])
+            def scale_and_store(batch):
+                n, b = batch
+                att, row_sum = state[batch]
+                inv_sum = stat_pool.tile([P, BATCH], F32)
+                nc.vector.tensor_reduce(
+                    out=inv_sum[:], in_=att[:, :, 0:ROWS], axis=X_AXIS, op=ALU.add
+                )
+                nc.vector.tensor_tensor(out=inv_sum[:], in0=inv_sum[:], in1=row_sum[:], op=ALU.add)
+                nc.vector.reciprocal(out=inv_sum[:], in_=inv_sum[:])
+                for t in range(BATCH):
+                    if t % SCALAR_EVERY == 0:
+                        nc.scalar.activation(
+                            out=att[:, t, :],
+                            in_=att[:, t, :],
+                            func=ACT.Copy,
+                            scale=inv_sum[:, t : t + 1],
+                        )
+                    else:
+                        nc.vector.tensor_scalar(
+                            out=att[:, t, :],
+                            in0=att[:, t, :],
+                            scalar1=inv_sum[:, t : t + 1],
+                            scalar2=None,
+                            op0=ALU.mult,
+                        )
+                for i in range(BATCH_ROWS):
+                    nc.sync.dma_start(
+                        out=out[0, n, b * BATCH_ROWS + i].rearrange("(s w) c -> w s c", s=HALVES),
+                        in_=att[:, i * HALVES : (i + 1) * HALVES, :],
+                    )
+
+            energies(batches[0])
+            exponentials(batches[0])
+            energies(batches[1])
+            for i in range(len(batches)):
+                if i + 1 < len(batches):
+                    exponentials(batches[i + 1])
+                scale_and_store(batches[i])
+                if i + 2 < len(batches):
+                    energies(batches[i + 2])

@@ -33,7 +33,6 @@ PSUM_BANKS = 8
 
 BATCH_ROWS = 4
 BATCH = BATCH_ROWS * HALVES
-SCALAR_EVERY = 3
 ATT_BUFS = 6
 
 FLOPS = 2 * HEADS * POSITIONS * KEYS * P * PACK
@@ -265,20 +264,29 @@ def tile_multiheadcrisscrossattention_pa_t_kernel(tc, q, k, out):
                 nc.vector.tensor_tensor(out=inv_sum[:], in0=inv_sum[:], in1=row_sum[:], op=ALU.add)
                 nc.vector.reciprocal(out=inv_sum[:], in_=inv_sum[:])
                 for t in range(BATCH):
-                    if t % SCALAR_EVERY == 0:
-                        nc.scalar.activation(
+                    if t % 2 == 1:
+                        nc.gpsimd.tensor_scalar(
                             out=att[:, t, :],
-                            in_=att[:, t, :],
-                            func=ACT.Copy,
-                            scale=inv_sum[:, t : t + 1],
+                            in0=att[:, t, :],
+                            scalar1=inv_sum[:, t : t + 1],
+                            scalar2=0.0,
+                            op0=ALU.mult,
+                            op1=ALU.add,
                         )
-                    else:
+                    elif t % 4 == 0:
                         nc.vector.tensor_scalar(
                             out=att[:, t, :],
                             in0=att[:, t, :],
                             scalar1=inv_sum[:, t : t + 1],
                             scalar2=None,
                             op0=ALU.mult,
+                        )
+                    else:
+                        nc.scalar.activation(
+                            out=att[:, t, :],
+                            in_=att[:, t, :],
+                            func=ACT.Copy,
+                            scale=inv_sum[:, t : t + 1],
                         )
                 for i in range(BATCH_ROWS):
                     nc.sync.dma_start(

@@ -33,6 +33,7 @@ PSUM_BANKS = 8
 
 BATCH_ROWS = 4
 BATCH = BATCH_ROWS * HALVES
+SCALAR_EVERY = 3
 ATT_BUFS = 6
 
 FLOPS = 2 * HEADS * POSITIONS * KEYS * P * PACK
@@ -44,6 +45,7 @@ def tile_multiheadcrisscrossattention_pa_t_kernel(tc, q, k, out):
         tc.tile_pool(name="keep", bufs=1) as keep,
         tc.tile_pool(name="stat_pool", bufs=4) as stat_pool,
         tc.psum_pool(name="psum", bufs=PSUM_BANKS) as psum,
+        tc.manual_schedule(),
     ):
         warm = keep.tile([P, 1], F32, name="warm")
         nc.vector.memset(warm[:], 0.0)
@@ -69,6 +71,84 @@ def tile_multiheadcrisscrossattention_pa_t_kernel(tc, q, k, out):
                 out=col_energy[n][:],
                 in_=out[0, n].rearrange("h (s w) c -> w (h s) c", s=HALVES)[:, :, 0:ROWS],
             )
+
+        neg_col_max = {}
+
+        def column_mask_and_max(n):
+            flat = col_energy[n][:].rearrange("p t j -> p (t j)")
+            for s in range(HALVES):
+                nc.gpsimd.memset(flat[:, s * ROWS :: HALVES * ROWS + 1], NEG_INF)
+            neg_col_max[n] = keep.tile([P, ROWS * HALVES], F32, name="neg_col_max_%d" % n)
+            nc.vector.tensor_reduce(
+                out=neg_col_max[n][:], in_=col_energy[n][:], axis=X_AXIS, op=ALU.max, negate=True
+            )
+
+        batches = [(n, b) for n in range(HEADS) for b in range(ROWS // BATCH_ROWS)]
+        tiles_of = {}
+
+        def begin(batch):
+            n, b = batch
+            if b == 0:
+                column_mask_and_max(n)
+            tiles_of[batch] = {
+                "row_banks": [],
+                "neg_row_max": stat_pool.tile([P, BATCH], F32, name="neg_row_max"),
+                "neg_max": stat_pool.tile([P, BATCH], F32, name="neg_max"),
+                "shifted": stat_pool.tile([P, BATCH, ROWS], F32, name="shifted"),
+            }
+
+        def row_maximum(batch, i):
+            n, b = batch
+            mine = tiles_of[batch]
+            h = b * BATCH_ROWS + i
+            row_bank = psum.tile([P, HALVES, COLS], F32, tag="bank")
+            for s in range(HALVES):
+                queries = slice(h * COLS + s * P, h * COLS + (s + 1) * P)
+                keys = slice(h * COLS, (h + 1) * COLS)
+                nc.tensor.matmul_mx(
+                    out=row_bank[:, s, :],
+                    lhsT=row_codes["q", n][:, queries].bitcast(FP8X4),
+                    lhsT_scale=row_scales["q", n][:, queries],
+                    rhs=row_codes["k", n][:, keys].bitcast(FP8X4),
+                    rhs_scale=row_scales["k", n][:, keys],
+                    start=True,
+                    stop=True,
+                )
+            nc.vector.tensor_reduce(
+                out=mine["neg_row_max"][:, i * HALVES : (i + 1) * HALVES],
+                in_=row_bank[:],
+                axis=X_AXIS,
+                op=ALU.max,
+                negate=True,
+            )
+            mine["row_banks"].append(row_bank)
+
+        def joint_maximum(batch):
+            n, b = batch
+            mine = tiles_of[batch]
+            nc.vector.tensor_tensor(
+                out=mine["neg_max"][:],
+                in0=mine["neg_row_max"][:],
+                in1=neg_col_max[n][:, b * BATCH : (b + 1) * BATCH],
+                op=ALU.min,
+            )
+
+        def shift_columns(batch):
+            n, b = batch
+            mine = tiles_of[batch]
+            nc.vector.tensor_tensor(
+                out=mine["shifted"][:],
+                in0=col_energy[n][:, b * BATCH : (b + 1) * BATCH, :],
+                in1=mine["neg_max"][:].unsqueeze(2).to_broadcast([P, BATCH, ROWS]),
+                op=ALU.add,
+            )
+
+        def start(batch):
+            begin(batch)
+            for i in range(BATCH_ROWS):
+                row_maximum(batch, i)
+            joint_maximum(batch)
+            shift_columns(batch)
 
         with (
             tc.tile_pool(name="raw_pool", bufs=RAW_BUFS) as raw_pool,
@@ -111,7 +191,7 @@ def tile_multiheadcrisscrossattention_pa_t_kernel(tc, q, k, out):
                     )
                 return grouped
 
-            def quantise_and_move(chunk, grouped):
+            def quantise(chunk, grouped):
                 n, name, source, c = chunk
                 positions = slice(c * CHUNK, (c + 1) * CHUNK)
                 nc.vector.quantize_mx(
@@ -119,6 +199,10 @@ def tile_multiheadcrisscrossattention_pa_t_kernel(tc, q, k, out):
                     scales=row_scales[name, n][:, positions],
                     in_=grouped[:].rearrange("p c t -> p (c t)"),
                 )
+
+            def move(chunk):
+                n, name, source, c = chunk
+                positions = slice(c * CHUNK, (c + 1) * CHUNK)
                 chunk_rows = slice(c * CHUNK_ROWS, (c + 1) * CHUNK_ROWS)
                 nc.vector.tensor_copy(
                     out=col_codes[name][:]
@@ -163,117 +247,72 @@ def tile_multiheadcrisscrossattention_pa_t_kernel(tc, q, k, out):
                     nc.sync.dma_start(out=by_u[u, :, :, 0:ROWS], in_=products[u:P:OCT, :, u, :])
 
             raws = [load(chunk) for chunk in chunks[: RAW_BUFS - 1]]
-            regrouped = None
-            for i in range(len(chunks) + 1):
+            regrouped = regroup(raws[0])
+            for i in range(len(chunks)):
                 if i + RAW_BUFS - 1 < len(chunks):
                     raws.append(load(chunks[i + RAW_BUFS - 1]))
-                previous = regrouped
-                if i < len(chunks):
-                    regrouped = regroup(raws[i])
-                if i > 0:
-                    quantise_and_move(chunks[i - 1], previous)
-                    if i % (len(chunks) // HEADS) == 0:
-                        n = chunks[i - 1][0]
-                        if n > 0:
-                            column_energies_back(n - 1)
-                        column_products(n)
+                quantise(chunks[i], regrouped)
+                if i + 1 < len(chunks):
+                    regrouped = regroup(raws[i + 1])
+                move(chunks[i])
+                if (i + 1) % (len(chunks) // HEADS) == 0:
+                    n = chunks[i][0]
+                    if n > 0:
+                        column_energies_back(n - 1)
+                    if n == HEADS - 1:
+                        start(batches[0])
+                    column_products(n)
 
         column_energies_back(HEADS - 1)
 
         with tc.tile_pool(name="att_pool", bufs=ATT_BUFS, reuse_waits="tile") as att_pool:
-            neg_col_max = {}
-
-            def column_mask_and_max(n):
-                flat = col_energy[n][:].rearrange("p t j -> p (t j)")
-                for s in range(HALVES):
-                    nc.gpsimd.memset(flat[:, s * ROWS :: HALVES * ROWS + 1], NEG_INF)
-                neg_col_max[n] = keep.tile([P, ROWS * HALVES], F32, name="neg_col_max_%d" % n)
-                nc.vector.tensor_reduce(
-                    out=neg_col_max[n][:], in_=col_energy[n][:], axis=X_AXIS, op=ALU.max, negate=True
-                )
-
-            batches = [(n, b) for n in range(HEADS) for b in range(ROWS // BATCH_ROWS)]
-            state = {}
-
-            def energies(batch):
-                n, b = batch
-                if b == 0:
-                    column_mask_and_max(n)
-                tiles = slice(b * BATCH, (b + 1) * BATCH)
-                neg_row_max = stat_pool.tile([P, BATCH], F32)
-                row_banks = []
-                for i in range(BATCH_ROWS):
-                    h = b * BATCH_ROWS + i
-                    row_bank = psum.tile([P, HALVES, COLS], F32, tag="bank")
-                    for s in range(HALVES):
-                        queries = slice(h * COLS + s * P, h * COLS + (s + 1) * P)
-                        keys = slice(h * COLS, (h + 1) * COLS)
-                        nc.tensor.matmul_mx(
-                            out=row_bank[:, s, :],
-                            lhsT=row_codes["q", n][:, queries].bitcast(FP8X4),
-                            lhsT_scale=row_scales["q", n][:, queries],
-                            rhs=row_codes["k", n][:, keys].bitcast(FP8X4),
-                            rhs_scale=row_scales["k", n][:, keys],
-                            start=True,
-                            stop=True,
-                        )
-                    nc.vector.tensor_reduce(
-                        out=neg_row_max[:, i * HALVES : (i + 1) * HALVES],
-                        in_=row_bank[:],
-                        axis=X_AXIS,
-                        op=ALU.max,
-                        negate=True,
-                    )
-                    row_banks.append(row_bank)
-                neg_max = stat_pool.tile([P, BATCH], F32)
-                nc.vector.tensor_tensor(
-                    out=neg_max[:], in0=neg_row_max[:], in1=neg_col_max[n][:, tiles], op=ALU.min
-                )
-                shifted = stat_pool.tile([P, BATCH, ROWS], F32)
-                nc.vector.tensor_tensor(
-                    out=shifted[:],
-                    in0=col_energy[n][:, tiles, :],
-                    in1=neg_max[:].unsqueeze(2).to_broadcast([P, BATCH, ROWS]),
-                    op=ALU.add,
-                )
-                state[batch] = (row_banks, neg_max, shifted)
-
             def exponentials(batch):
-                row_banks, neg_max, shifted = state[batch]
+                mine = tiles_of[batch]
                 att = att_pool.tile([P, BATCH, KEYS], F32)
-                nc.scalar.activation(out=att[:, :, 0:ROWS], in_=shifted[:], func=ACT.Exp)
+                nc.scalar.activation(out=att[:, :, 0:ROWS], in_=mine["shifted"][:], func=ACT.Exp)
                 row_sum = stat_pool.tile([P, BATCH], F32)
                 for t in range(BATCH):
                     nc.scalar.activation(
                         out=att[:, t, ROWS:KEYS],
-                        in_=row_banks[t // HALVES][:, t % HALVES, :],
+                        in_=mine["row_banks"][t // HALVES][:, t % HALVES, :],
                         func=ACT.Exp,
-                        bias=neg_max[:, t : t + 1],
+                        bias=mine["neg_max"][:, t : t + 1],
                         scale=1.0,
                         accum_out=row_sum[:, t : t + 1],
                     )
-                state[batch] = (att, row_sum)
+                mine["att"] = att
+                mine["row_sum"] = row_sum
+                mine["inv_sum"] = stat_pool.tile([P, BATCH], F32, name="inv_sum")
 
-            def scale_and_store(batch):
-                n, b = batch
-                att, row_sum = state[batch]
-                inv_sum = stat_pool.tile([P, BATCH], F32)
+            def sum_columns(batch):
+                mine = tiles_of[batch]
                 nc.vector.tensor_reduce(
-                    out=inv_sum[:], in_=att[:, :, 0:ROWS], axis=X_AXIS, op=ALU.add
+                    out=mine["inv_sum"][:], in_=mine["att"][:, :, 0:ROWS], axis=X_AXIS, op=ALU.add
                 )
-                nc.vector.tensor_tensor(out=inv_sum[:], in0=inv_sum[:], in1=row_sum[:], op=ALU.add)
-                nc.vector.reciprocal(out=inv_sum[:], in_=inv_sum[:])
-                for t in range(BATCH):
-                    if t % 2 == 1:
-                        nc.gpsimd.tensor_scalar(
+
+            def add_sums(batch):
+                mine = tiles_of[batch]
+                nc.vector.tensor_tensor(
+                    out=mine["inv_sum"][:], in0=mine["inv_sum"][:], in1=mine["row_sum"][:], op=ALU.add
+                )
+
+            def invert(batch):
+                mine = tiles_of[batch]
+                nc.vector.reciprocal(out=mine["inv_sum"][:], in_=mine["inv_sum"][:])
+
+            def scale_and_store(batch, i):
+                n, b = batch
+                att = tiles_of[batch]["att"]
+                inv_sum = tiles_of[batch]["inv_sum"]
+                for t in range(i * HALVES, (i + 1) * HALVES):
+                    if t % SCALAR_EVERY == 0:
+                        nc.scalar.activation(
                             out=att[:, t, :],
-                            in0=att[:, t, :],
-                            scalar1=inv_sum[:, t : t + 1],
-                            scalar2=0.0,
-                            op0=ALU.mult,
-                            op1=ALU.add,
+                            in_=att[:, t, :],
+                            func=ACT.Copy,
+                            scale=inv_sum[:, t : t + 1],
                         )
-                    elif t % 4 == 0:
+                    else:
                         nc.vector.tensor_scalar(
                             out=att[:, t, :],
                             in0=att[:, t, :],
@@ -281,25 +320,37 @@ def tile_multiheadcrisscrossattention_pa_t_kernel(tc, q, k, out):
                             scalar2=None,
                             op0=ALU.mult,
                         )
-                    else:
-                        nc.scalar.activation(
-                            out=att[:, t, :],
-                            in_=att[:, t, :],
-                            func=ACT.Copy,
-                            scale=inv_sum[:, t : t + 1],
-                        )
-                for i in range(BATCH_ROWS):
-                    nc.sync.dma_start(
-                        out=out[0, n, b * BATCH_ROWS + i].rearrange("(s w) c -> w s c", s=HALVES),
-                        in_=att[:, i * HALVES : (i + 1) * HALVES, :],
-                    )
+                nc.sync.dma_start(
+                    out=out[0, n, b * BATCH_ROWS + i].rearrange("(s w) c -> w s c", s=HALVES),
+                    in_=att[:, i * HALVES : (i + 1) * HALVES, :],
+                )
 
-            energies(batches[0])
+            start(batches[1])
             exponentials(batches[0])
-            energies(batches[1])
             for i in range(len(batches)):
+                done = batches[i]
+                more = i + 2 < len(batches)
+                ahead = batches[i + 2] if more else None
                 if i + 1 < len(batches):
                     exponentials(batches[i + 1])
-                scale_and_store(batches[i])
-                if i + 2 < len(batches):
-                    energies(batches[i + 2])
+                if more:
+                    begin(ahead)
+                sum_columns(done)
+                if more:
+                    row_maximum(ahead, 0)
+                add_sums(done)
+                if more:
+                    row_maximum(ahead, 1)
+                invert(done)
+                if more:
+                    row_maximum(ahead, 2)
+                scale_and_store(done, 0)
+                scale_and_store(done, 1)
+                if more:
+                    row_maximum(ahead, 3)
+                scale_and_store(done, 2)
+                if more:
+                    joint_maximum(ahead)
+                scale_and_store(done, 3)
+                if more:
+                    shift_columns(ahead)

@@ -23,7 +23,7 @@ NEG_INF = -1.0e9
 CHUNK_ROWS = 4
 CHUNK = CHUNK_ROWS * COLS
 RAW_BUFS = 5
-RUN = 4
+RUN = 8
 VECTOR_SHARE = 3 * CHUNK // 8
 
 OCT = 8

@@ -65,22 +65,30 @@ def tile_multiheadcrisscrossattention_pa_t_kernel(tc, q, k, out):
 
         col_energy = {}
 
+        def scratch(n):
+            flat = out[0, n, 0].rearrange("w c -> (w c)")
+            return flat[0 : COLS * ROWS * ROWS].rearrange("(w h j) -> w h j", h=ROWS, j=ROWS)
+
         def column_energies_back(n):
-            col_energy[n] = keep.tile([P, ROWS * HALVES, ROWS], F32, name="col_energy_%d" % n)
+            col_energy[n] = keep.tile([P, HALVES, ROWS, ROWS], F32, name="col_energy_%d" % n)
             nc.sync.dma_start(
-                out=col_energy[n][:],
-                in_=out[0, n].rearrange("h (s w) c -> w (h s) c", s=HALVES)[:, :, 0:ROWS],
+                out=col_energy[n][:].rearrange("p s h j -> p s (h j)"),
+                in_=scratch(n).rearrange("(s w) h j -> w s (h j)", s=HALVES),
             )
 
         neg_col_max = {}
 
         def column_mask_and_max(n):
-            flat = col_energy[n][:].rearrange("p t j -> p (t j)")
             for s in range(HALVES):
-                nc.gpsimd.memset(flat[:, s * ROWS :: HALVES * ROWS + 1], NEG_INF)
-            neg_col_max[n] = keep.tile([P, ROWS * HALVES], F32, name="neg_col_max_%d" % n)
+                flat = col_energy[n][:, s, :, :].rearrange("p h j -> p (h j)")
+                nc.gpsimd.memset(flat[:, :: ROWS + 1], NEG_INF)
+            neg_col_max[n] = keep.tile([P, ROWS, HALVES], F32, name="neg_col_max_%d" % n)
             nc.vector.tensor_reduce(
-                out=neg_col_max[n][:], in_=col_energy[n][:], axis=X_AXIS, op=ALU.max, negate=True
+                out=neg_col_max[n][:],
+                in_=col_energy[n][:].rearrange("p s h j -> p h s j"),
+                axis=X_AXIS,
+                op=ALU.max,
+                negate=True,
             )
 
         batches = [(n, b) for n in range(HEADS) for b in range(ROWS // BATCH_ROWS)]
@@ -129,7 +137,7 @@ def tile_multiheadcrisscrossattention_pa_t_kernel(tc, q, k, out):
             nc.vector.tensor_tensor(
                 out=mine["neg_max"][:],
                 in0=mine["neg_row_max"][:],
-                in1=neg_col_max[n][:, b * BATCH : (b + 1) * BATCH],
+                in1=neg_col_max[n][:, b * BATCH_ROWS : (b + 1) * BATCH_ROWS, :].rearrange("p h s -> p (h s)"),
                 op=ALU.min,
             )
 
@@ -137,9 +145,12 @@ def tile_multiheadcrisscrossattention_pa_t_kernel(tc, q, k, out):
             n, b = batch
             mine = tiles_of[batch]
             nc.vector.tensor_tensor(
-                out=mine["shifted"][:],
-                in0=col_energy[n][:, b * BATCH : (b + 1) * BATCH, :],
-                in1=mine["neg_max"][:].unsqueeze(2).to_broadcast([P, BATCH, ROWS]),
+                out=mine["shifted"][:].rearrange("p (h s) j -> p h s j", s=HALVES),
+                in0=col_energy[n][:, :, b * BATCH_ROWS : (b + 1) * BATCH_ROWS, :].rearrange("p s h j -> p h s j"),
+                in1=mine["neg_max"][:]
+                .rearrange("p (h s) -> p h s", s=HALVES)
+                .unsqueeze(3)
+                .to_broadcast([P, BATCH_ROWS, HALVES, ROWS]),
                 op=ALU.add,
             )
 
@@ -242,9 +253,9 @@ def tile_multiheadcrisscrossattention_pa_t_kernel(tc, q, k, out):
                         out=products[:, b * BANK_OCTETS : (b + 1) * BANK_OCTETS, :, :],
                         in_=col_bank[:].rearrange("p g (j u) -> p g u j", u=OCT),
                     )
-                by_u = out[0, n].rearrange("h (g u) c -> u h g c", u=OCT)
+                by_u = scratch(n).rearrange("(g u) h j -> u h g j", u=OCT)
                 for u in range(OCT):
-                    nc.sync.dma_start(out=by_u[u, :, :, 0:ROWS], in_=products[u:P:OCT, :, u, :])
+                    nc.sync.dma_start(out=by_u[u], in_=products[u:P:OCT, :, u, :])
 
             raws = [load(chunk) for chunk in chunks[: RAW_BUFS - 1]]
             regrouped = regroup(raws[0])

@@ -33,7 +33,8 @@ PSUM_BANKS = 8
 
 BATCH_ROWS = 4
 BATCH = BATCH_ROWS * HALVES
-SCALAR_EVERY = 3
+SCALAR_EVERY = 4
+VECTOR_ONLY_BATCHES = 3
 ATT_BUFS = 6
 
 FLOPS = 2 * HEADS * POSITIONS * KEYS * P * PACK
@@ -248,7 +249,7 @@ def tile_multiheadcrisscrossattention_pa_t_kernel(tc, q, k, out):
                             start=True,
                             stop=True,
                         )
-                    copy = nc.scalar.copy if b % 2 == 0 else nc.vector.tensor_copy
+                    copy = nc.scalar.copy if (b % 2 == 0 or n == HEADS - 1) else nc.vector.tensor_copy
                     copy(
                         out=products[:, b * BANK_OCTETS : (b + 1) * BANK_OCTETS, :, :],
                         in_=col_bank[:].rearrange("p g (j u) -> p g u j", u=OCT),
@@ -316,7 +317,7 @@ def tile_multiheadcrisscrossattention_pa_t_kernel(tc, q, k, out):
                 att = tiles_of[batch]["att"]
                 inv_sum = tiles_of[batch]["inv_sum"]
                 for t in range(i * HALVES, (i + 1) * HALVES):
-                    if t % SCALAR_EVERY == 0:
+                    if t % SCALAR_EVERY == 0 and batch in batches[:-VECTOR_ONLY_BATCHES]:
                         nc.scalar.activation(
                             out=att[:, t, :],
                             in_=att[:, t, :],

import concourse.mybir as mybir

BF16 = mybir.dt.bfloat16
F32 = mybir.dt.float32
I32 = mybir.dt.int32
U32 = mybir.dt.uint32
U8 = mybir.dt.uint8
FP8X4 = mybir.dt.float8_e4m3fn_x4
ALU = mybir.AluOpType
ACT = mybir.ActivationFunctionType
X_AXIS = mybir.AxisListType.X

P = 128
PACK = 4
HEADS = 2
ROWS = 16
COLS = 256
POSITIONS = ROWS * COLS
KEYS = ROWS + COLS
HALVES = COLS // P
NEG_INF = -1.0e9

CHUNK_ROWS = 4
CHUNK = CHUNK_ROWS * COLS
RAW_BUFS = 5
RUN = 8
VECTOR_SHARE = 3 * CHUNK // 8

OCT = 8
OCTETS = COLS // OCT
BANK_OCTETS = 4
PSUM_BANKS = 8

BATCH_ROWS = 4
BATCH = BATCH_ROWS * HALVES
SCALAR_EVERY = 4
VECTOR_ONLY_BATCHES = 3
ATT_BUFS = 6

FLOPS = 2 * HEADS * POSITIONS * KEYS * P * PACK


def tile_multiheadcrisscrossattention_pa_t_kernel(tc, q, k, out):
    nc = tc.nc
    with (
        tc.tile_pool(name="keep", bufs=1) as keep,
        tc.tile_pool(name="stat_pool", bufs=4) as stat_pool,
        tc.psum_pool(name="psum", bufs=PSUM_BANKS) as psum,
        tc.manual_schedule(),
    ):
        warm = keep.tile([P, 1], F32, name="warm")
        nc.vector.memset(warm[:], 0.0)
        nc.scalar.activation(out=warm[:], in_=warm[:], func=ACT.Exp)

        row_codes = {}
        row_scales = {}
        for n in range(HEADS):
            for name in ("q", "k"):
                row_codes[name, n] = keep.tile(
                    [P, POSITIONS], U32, align_bytes=64, name="row_codes_%s%d" % (name, n)
                )
                row_scales[name, n] = keep.tile(
                    [P, POSITIONS], U8, align_bytes=64, name="row_scales_%s%d" % (name, n)
                )
                nc.vector.memset(row_scales[name, n][:].bitcast(I32), 0)

        col_energy = {}

        def scratch(n):
            flat = out[0, n, 0].rearrange("w c -> (w c)")
            return flat[0 : COLS * ROWS * ROWS].rearrange("(w h j) -> w h j", h=ROWS, j=ROWS)

        def column_energies_back(n):
            col_energy[n] = keep.tile([P, HALVES, ROWS, ROWS], F32, name="col_energy_%d" % n)
            nc.sync.dma_start(
                out=col_energy[n][:].rearrange("p s h j -> p s (h j)"),
                in_=scratch(n).rearrange("(s w) h j -> w s (h j)", s=HALVES),
            )

        neg_col_max = {}

        def column_mask_and_max(n):
            for s in range(HALVES):
                flat = col_energy[n][:, s, :, :].rearrange("p h j -> p (h j)")
                nc.gpsimd.memset(flat[:, :: ROWS + 1], NEG_INF)
            neg_col_max[n] = keep.tile([P, ROWS, HALVES], F32, name="neg_col_max_%d" % n)
            nc.vector.tensor_reduce(
                out=neg_col_max[n][:],
                in_=col_energy[n][:].rearrange("p s h j -> p h s j"),
                axis=X_AXIS,
                op=ALU.max,
                negate=True,
            )

        batches = [(n, b) for n in range(HEADS) for b in range(ROWS // BATCH_ROWS)]
        tiles_of = {}

        def begin(batch):
            n, b = batch
            if b == 0:
                column_mask_and_max(n)
            tiles_of[batch] = {
                "row_banks": [],
                "neg_row_max": stat_pool.tile([P, BATCH], F32, name="neg_row_max"),
                "neg_max": stat_pool.tile([P, BATCH], F32, name="neg_max"),
                "shifted": stat_pool.tile([P, BATCH, ROWS], F32, name="shifted"),
            }

        def row_maximum(batch, i):
            n, b = batch
            mine = tiles_of[batch]
            h = b * BATCH_ROWS + i
            row_bank = psum.tile([P, HALVES, COLS], F32, tag="bank")
            for s in range(HALVES):
                queries = slice(h * COLS + s * P, h * COLS + (s + 1) * P)
                keys = slice(h * COLS, (h + 1) * COLS)
                nc.tensor.matmul_mx(
                    out=row_bank[:, s, :],
                    lhsT=row_codes["q", n][:, queries].bitcast(FP8X4),
                    lhsT_scale=row_scales["q", n][:, queries],
                    rhs=row_codes["k", n][:, keys].bitcast(FP8X4),
                    rhs_scale=row_scales["k", n][:, keys],
                    start=True,
                    stop=True,
                )
            nc.vector.tensor_reduce(
                out=mine["neg_row_max"][:, i * HALVES : (i + 1) * HALVES],
                in_=row_bank[:],
                axis=X_AXIS,
                op=ALU.max,
                negate=True,
            )
            mine["row_banks"].append(row_bank)

        def joint_maximum(batch):
            n, b = batch
            mine = tiles_of[batch]
            nc.vector.tensor_tensor(
                out=mine["neg_max"][:],
                in0=mine["neg_row_max"][:],
                in1=neg_col_max[n][:, b * BATCH_ROWS : (b + 1) * BATCH_ROWS, :].rearrange("p h s -> p (h s)"),
                op=ALU.min,
            )

        def shift_columns(batch):
            n, b = batch
            mine = tiles_of[batch]
            nc.vector.tensor_tensor(
                out=mine["shifted"][:].rearrange("p (h s) j -> p h s j", s=HALVES),
                in0=col_energy[n][:, :, b * BATCH_ROWS : (b + 1) * BATCH_ROWS, :].rearrange("p s h j -> p h s j"),
                in1=mine["neg_max"][:]
                .rearrange("p (h s) -> p h s", s=HALVES)
                .unsqueeze(3)
                .to_broadcast([P, BATCH_ROWS, HALVES, ROWS]),
                op=ALU.add,
            )

        def start(batch):
            begin(batch)
            for i in range(BATCH_ROWS):
                row_maximum(batch, i)
            joint_maximum(batch)
            shift_columns(batch)

        with (
            tc.tile_pool(name="raw_pool", bufs=RAW_BUFS) as raw_pool,
            tc.tile_pool(name="grouped_pool", bufs=4) as grouped_pool,
            tc.tile_pool(name="col_pool", bufs=1) as col_pool,
        ):
            col_codes = {}
            col_scales = {}
            for name in ("q", "k"):
                col_codes[name] = col_pool.tile(
                    [P, POSITIONS], U32, align_bytes=64, name="col_codes_%s" % name
                )
                col_scales[name] = col_pool.tile(
                    [P, POSITIONS], U8, align_bytes=64, name="col_scales_%s" % name
                )

            chunks = [
                (n, name, source, c)
                for n in range(HEADS)
                for name, source in (("q", q), ("k", k))
                for c in range(ROWS // CHUNK_ROWS)
            ]

            def load(chunk):
                n, name, source, c = chunk
                channels = source[0, n].rearrange("(p t) h w -> p t (h w)", t=PACK)
                raw = raw_pool.tile([P, PACK, CHUNK], BF16)
                nc.sync.dma_start(out=raw[:], in_=channels[:, :, c * CHUNK : (c + 1) * CHUNK])
                return raw

            def regroup(raw):
                grouped = grouped_pool.tile([P, CHUNK, PACK], BF16, align_bytes=64)
                for copy, share in (
                    (nc.vector.tensor_copy, slice(0, VECTOR_SHARE)),
                    (nc.scalar.copy, slice(VECTOR_SHARE, CHUNK)),
                ):
                    copy(
                        out=grouped[:, share, :].rearrange("p (c i) t -> p c t i", i=RUN),
                        in_=raw[:, :, share].rearrange("p t (c i) -> p c t i", i=RUN),
                    )
                return grouped

            def quantise(chunk, grouped):
                n, name, source, c = chunk
                positions = slice(c * CHUNK, (c + 1) * CHUNK)
                nc.vector.quantize_mx(
                    out=row_codes[name, n][:, positions].bitcast(FP8X4),
                    scales=row_scales[name, n][:, positions],
                    in_=grouped[:].rearrange("p c t -> p (c t)"),
                )

            def move(chunk):
                n, name, source, c = chunk
                positions = slice(c * CHUNK, (c + 1) * CHUNK)
                chunk_rows = slice(c * CHUNK_ROWS, (c + 1) * CHUNK_ROWS)
                nc.vector.tensor_copy(
                    out=col_codes[name][:]
                    .bitcast(I32)
                    .rearrange("p (g h u) -> p g h u", h=ROWS, u=OCT)[:, :, chunk_rows, :],
                    in_=row_codes[name, n][:, positions]
                    .bitcast(I32)
                    .rearrange("p (h g u) -> p g h u", g=OCTETS, u=OCT),
                )
                nc.vector.tensor_copy(
                    out=col_scales[name][:]
                    .bitcast(I32)
                    .rearrange("p (g h e) -> p g h e", h=ROWS, e=OCT // 4)[:, :, chunk_rows, :],
                    in_=row_scales[name, n][:, positions]
                    .bitcast(I32)
                    .rearrange("p (h g e) -> p g h e", g=OCTETS, e=OCT // 4),
                )

            def column_products(n):
                products = col_pool.tile([P, OCTETS, OCT, ROWS], F32)
                for b in range(OCTETS // BANK_OCTETS):
                    col_bank = psum.tile([P, BANK_OCTETS, P], F32, tag="bank")
                    for i in range(BANK_OCTETS):
                        g = b * BANK_OCTETS + i
                        octet = slice(g * P, (g + 1) * P)
                        nc.tensor.matmul_mx(
                            out=col_bank[:, i, :],
                            lhsT=col_codes["q"][:, octet].bitcast(FP8X4),
                            lhsT_scale=col_scales["q"][:, octet],
                            rhs=col_codes["k"][:, octet].bitcast(FP8X4),
                            rhs_scale=col_scales["k"][:, octet],
                            start=True,
                            stop=True,
                        )
                    copy = nc.scalar.copy if (b % 2 == 0 or n == HEADS - 1) else nc.vector.tensor_copy
                    copy(
                        out=products[:, b * BANK_OCTETS : (b + 1) * BANK_OCTETS, :, :],
                        in_=col_bank[:].rearrange("p g (j u) -> p g u j", u=OCT),
                    )
                by_u = scratch(n).rearrange("(g u) h j -> u h g j", u=OCT)
                for u in range(OCT):
                    nc.sync.dma_start(out=by_u[u], in_=products[u:P:OCT, :, u, :])

            raws = [load(chunk) for chunk in chunks[: RAW_BUFS - 1]]
            regrouped = regroup(raws[0])
            for i in range(len(chunks)):
                if i + RAW_BUFS - 1 < len(chunks):
                    raws.append(load(chunks[i + RAW_BUFS - 1]))
                quantise(chunks[i], regrouped)
                if i + 1 < len(chunks):
                    regrouped = regroup(raws[i + 1])
                move(chunks[i])
                if (i + 1) % (len(chunks) // HEADS) == 0:
                    n = chunks[i][0]
                    if n > 0:
                        column_energies_back(n - 1)
                    if n == HEADS - 1:
                        start(batches[0])
                    column_products(n)

        column_energies_back(HEADS - 1)

        with tc.tile_pool(name="att_pool", bufs=ATT_BUFS, reuse_waits="tile") as att_pool:
            def exponentials(batch):
                mine = tiles_of[batch]
                att = att_pool.tile([P, BATCH, KEYS], F32)
                nc.scalar.activation(out=att[:, :, 0:ROWS], in_=mine["shifted"][:], func=ACT.Exp)
                row_sum = stat_pool.tile([P, BATCH], F32)
                for t in range(BATCH):
                    nc.scalar.activation(
                        out=att[:, t, ROWS:KEYS],
                        in_=mine["row_banks"][t // HALVES][:, t % HALVES, :],
                        func=ACT.Exp,
                        bias=mine["neg_max"][:, t : t + 1],
                        scale=1.0,
                        accum_out=row_sum[:, t : t + 1],
                    )
                mine["att"] = att
                mine["row_sum"] = row_sum
                mine["inv_sum"] = stat_pool.tile([P, BATCH], F32, name="inv_sum")

            def sum_columns(batch):
                mine = tiles_of[batch]
                nc.vector.tensor_reduce(
                    out=mine["inv_sum"][:], in_=mine["att"][:, :, 0:ROWS], axis=X_AXIS, op=ALU.add
                )

            def add_sums(batch):
                mine = tiles_of[batch]
                nc.vector.tensor_tensor(
                    out=mine["inv_sum"][:], in0=mine["inv_sum"][:], in1=mine["row_sum"][:], op=ALU.add
                )

            def invert(batch):
                mine = tiles_of[batch]
                nc.vector.reciprocal(out=mine["inv_sum"][:], in_=mine["inv_sum"][:])

            def scale_and_store(batch, i):
                n, b = batch
                att = tiles_of[batch]["att"]
                inv_sum = tiles_of[batch]["inv_sum"]
                for t in range(i * HALVES, (i + 1) * HALVES):
                    if t % SCALAR_EVERY == 0 and batch in batches[:-VECTOR_ONLY_BATCHES]:
                        nc.scalar.activation(
                            out=att[:, t, :],
                            in_=att[:, t, :],
                            func=ACT.Copy,
                            scale=inv_sum[:, t : t + 1],
                        )
                    else:
                        nc.vector.tensor_scalar(
                            out=att[:, t, :],
                            in0=att[:, t, :],
                            scalar1=inv_sum[:, t : t + 1],
                            scalar2=None,
                            op0=ALU.mult,
                        )
                nc.sync.dma_start(
                    out=out[0, n, b * BATCH_ROWS + i].rearrange("(s w) c -> w s c", s=HALVES),
                    in_=att[:, i * HALVES : (i + 1) * HALVES, :],
                )

            start(batches[1])
            exponentials(batches[0])
            for i in range(len(batches)):
                done = batches[i]
                more = i + 2 < len(batches)
                ahead = batches[i + 2] if more else None
                if i + 1 < len(batches):
                    exponentials(batches[i + 1])
                if more:
                    begin(ahead)
                sum_columns(done)
                if more:
                    row_maximum(ahead, 0)
                add_sums(done)
                if more:
                    row_maximum(ahead, 1)
                invert(done)
                if more:
                    row_maximum(ahead, 2)
                scale_and_store(done, 0)
                scale_and_store(done, 1)
                if more:
                    row_maximum(ahead, 3)
                scale_and_store(done, 2)
                if more:
                    joint_maximum(ahead)
                scale_and_store(done, 3)
                if more:
                    shift_columns(ahead)
